import numpy as np
import ml_dtypes


def mxq(x, axis, fmt="e4m3"):
    dtype, down = {"e4m3": (ml_dtypes.float8_e4m3fn, 7), "e5m2": (ml_dtypes.float8_e5m2, 14)}[fmt]
    v = np.moveaxis(np.asarray(x, np.float32).astype(ml_dtypes.bfloat16).astype(np.float64), axis, -1)
    blocks = v.reshape(v.shape[:-1] + (-1, 32))
    amax = np.abs(blocks).max(-1, keepdims=True)
    byte = np.maximum(np.where(amax > 0, np.frexp(amax)[1] - 1 + 127, 0) - down, 1)
    scale = np.exp2(byte - 127.0)
    codes = (blocks / scale).astype(np.float32).astype(dtype).astype(np.float64)
    return np.moveaxis((codes * scale).reshape(v.shape), -1, axis)


WIDE = False


def mx_kscale(k):
    if not WIDE:
        return np.ones(k)
    levels = np.array([10, -10, 5, -5, 0])
    if k % 512:
        return np.exp2(np.random.permutation(np.resize(levels, k // 32))).repeat(32)
    a = np.empty((k // 512, 16))
    for p in range(k // 512):
        a[p, :8] = np.random.permutation(np.resize(levels, 8))
        for g in range(8):
            far = levels[np.abs(levels - a[p, g]) >= 10]
            a[p, g + 8] = far[np.random.randint(len(far))]
    return np.exp2(a.ravel()).repeat(32)


BF16 = ml_dtypes.bfloat16


def bf(x):
    return np.asarray(x, np.float32).astype(BF16)


def f64(x):
    return np.asarray(x).astype(np.float64)


B, S, D_IN, D_OUT, R = 4, 2048, 1024, 512, 128
LORA_SCALE = 2.0


def setup_inputs():
    s = mx_kscale(D_IN)
    return {"x": bf(np.random.standard_normal((B, S, D_IN)) * s),
            "weight": bf(np.random.standard_normal((D_OUT, D_IN)) * 1.0 / np.sqrt(D_IN) / s),
            "bias": bf(np.random.standard_normal(D_OUT) * 0.5),
            "lora_left": bf(np.random.standard_normal((D_OUT, R)) * 0.5 / np.sqrt(R)),
            "lora_right": bf(np.random.standard_normal((R, D_IN)) * 0.5 / np.sqrt(D_IN) / s)}


def reference(x, weight, bias, lora_left, lora_right):
    w_eff = f64(weight) + LORA_SCALE * (f64(lora_left) @ f64(lora_right))
    return (mxq(f64(x), 2, "e4m3") @ mxq(w_eff, 1, "e4m3").T) + f64(bias)

@@ -1,0 +1,207 @@
+from contextlib import ExitStack
+
+import concourse.masks as masks
+import concourse.mybir as mybir
+
+F32 = mybir.dt.float32
+BF16 = mybir.dt.bfloat16
+U32 = mybir.dt.uint32
+U8 = mybir.dt.uint8
+FP8X4 = mybir.dt.float8_e4m3fn_x4
+ADD = mybir.AluOpType.add
+
+P = 128
+ROWS = 8192
+D_IN = 1024
+D_OUT = 512
+RANK = 128
+LORA_SCALE = 2.0
+J = 8
+SLABS = ROWS // (P * J)
+BUNCH_SIZES = [4, 4] + [8] * 7
+MAX_BUNCH = 8
+FINE_SLABS = 2
+WARM_UP = 4
+GP_EVERY = 4
+FLOPS = 2 * ROWS * D_IN * D_OUT + 2 * D_OUT * RANK * D_IN
+
+
+def tile_loralinear_t_kernel(tc, x, weight, bias, lora_left, lora_right, out):
+    nc = tc.nc
+    xv = x.flatten_outer_dims().rearrange("(s p j) k -> s p (j k)", p=P, j=J)
+    ov = out.flatten_outer_dims().rearrange("(s p j) o -> s p (j o)", p=P, j=J)
+    with ExitStack() as ctx:
+        const = ctx.enter_context(tc.tile_pool(name="const", bufs=1))
+        slabs = ctx.enter_context(tc.tile_pool(name="slabs", bufs=9))
+        work = ctx.enter_context(tc.tile_pool(name="work", bufs=2))
+        psum = ctx.enter_context(tc.psum_pool(name="psum", bufs=8))
+        ctx.enter_context(tc.manual_schedule())
+
+        ident_bf = const.tile([P, P], BF16, name="ident_bf")
+        masks.make_identity(nc, ident_bf[:])
+        ident_f = const.tile([P, P], F32, name="ident_f")
+        masks.make_identity(nc, ident_f[:])
+        ones = const.tile([P, P], BF16, name="ones")
+        nc.vector.memset(ones[:], 1.0)
+        warm = const.tile([P, D_OUT], BF16, name="warm")
+        nc.vector.memset(warm[:], 0.0)
+        bias_row = const.tile([P, D_OUT], BF16, name="bias_row")
+        nc.vector.memset(bias_row[:], 0.0)
+        pd = psum.tile([P, D_OUT], F32, name="pd", tag="bank")
+        for n in range(WARM_UP):
+            nc.tensor.matmul(pd[:], lhsT=ones[:], rhs=warm[:], start=True, stop=True)
+
+        ll_sb = const.tile([P, 4, RANK], BF16, name="ll_sb")
+        nc.sync.dma_start(out=ll_sb[:], in_=lora_left.rearrange("(t p) r -> p t r", p=P))
+        lr_sb = const.tile([P, D_IN], BF16, name="lr_sb")
+        nc.sync.dma_start(out=lr_sb[:], in_=lora_right)
+        nc.sync.dma_start(out=bias_row[0:1, :], in_=bias.unsqueeze(0))
+        w_sb = const.tile([P, 2, 4, 512], BF16, name="w_sb")
+        w_dram = weight.rearrange("(t p) (g k) -> g p t k", p=P, g=2)
+        x_tiles = []
+        for s in range(SLABS):
+            x_slab = slabs.tile([P, J * D_IN], BF16, name="x_slab", tag="slab")
+            x_tiles.append(x_slab)
+        half = J * D_IN // 2
+        for t in range(4):
+            nc.sync.dma_start(out=w_sb[:, 0, t], in_=w_dram[0][:, t])
+        nc.sync.dma_start(out=x_tiles[0][:, 0:half], in_=xv[0][:, 0:half])
+        nc.sync.dma_start(out=w_sb[:, 1], in_=w_dram[1])
+        nc.sync.dma_start(out=x_tiles[0][:, half : 2 * half], in_=xv[0][:, half : 2 * half])
+        for s in range(1, SLABS):
+            nc.sync.dma_start(out=x_tiles[s][:], in_=xv[s])
+
+        pl = psum.tile([P, 4, P], BF16, name="pl", tag="bank")
+        for t in range(4):
+            nc.tensor.transpose(pl[:, t, :], ll_sb[:, t, :], ident_bf[:])
+        ll_t2 = const.tile([P, D_OUT], BF16, name="ll_t2")
+        nc.vector.tensor_scalar_mul(out=ll_t2[:], in0=pl[:].rearrange("p t o -> p (t o)"), scalar1=LORA_SCALE)
+
+        bias_sb = const.tile([P, D_OUT], F32, name="bias_sb")
+
+        w_view = w_sb[:].rearrange("p g t (q v) -> p g t q v", q=P, v=4)
+        lr_view = lr_sb[:].rearrange("p (g q v) -> p g q v", g=2, q=P, v=4)
+        wg = const.tile([P, 2, D_OUT, 4], BF16, name="wg", align_bytes=64)
+        wc = const.tile([P, 2 * D_OUT], U32, name="wc", align_bytes=64)
+        ws = const.tile([P, 2 * D_OUT], U8, name="ws", align_bytes=64)
+
+        def weight_bank(g, t, on_vector):
+            pw = psum.tile([P, 4, P], F32, name="pw", tag="bank")
+            for v in range(4):
+                nc.tensor.matmul(pw[:, v, :], lhsT=w_view[:, g, t, :, v], rhs=ident_bf[:], start=True, stop=False)
+                nc.tensor.matmul(
+                    pw[:, v, :], lhsT=lr_view[:, g, :, v], rhs=ll_t2[:, t * P : (t + 1) * P], start=False, stop=True
+                )
+            dst = wg[:, g, t * P : (t + 1) * P, :]
+            src = pw[:].rearrange("p v o -> p o v")
+            if on_vector:
+                nc.vector.tensor_copy(out=dst, in_=src)
+            else:
+                nc.scalar.copy(out=dst, in_=src)
+
+        def weight_quantise(g):
+            cols = slice(g * D_OUT, (g + 1) * D_OUT)
+            nc.vector.quantize_mx(
+                out=wc[:, cols].bitcast(FP8X4), scales=ws[:, cols], in_=wg[:, g].rearrange("p o v -> p (o v)")
+            )
+
+        bunches = []
+        first = 0
+        for size in BUNCH_SIZES:
+            bunches.append(list(range(first, first + size)))
+            first += size
+        assert first == ROWS // P
+        groups = {}
+        codes = {}
+        o_tiles = {}
+
+        def transposes(b):
+            tiles = bunches[b]
+            grp = work.tile([P, MAX_BUNCH * 1024], BF16, name="grp", tag="grp", align_bytes=64)
+            gw = grp[:].bitcast(F32).rearrange("p (i g r u) -> p i g r u", i=MAX_BUNCH, g=2, r=P, u=2)
+            for i, rt in enumerate(tiles):
+                s, j = divmod(rt, J)
+                xw = x_tiles[s][:].bitcast(F32)
+                tb = psum.tile([P, 4, P], F32, name="tb", tag="bank")
+                for c in range(4):
+                    g, u = divmod(c, 2)
+                    w0 = j * 512 + g * 256
+                    nc.tensor.transpose(tb[:, c, :], xw[:, w0 + u : w0 + 256 : 2], ident_f[:])
+                nc.scalar.copy(out=gw[:, i], in_=tb[:].rearrange("p (g u) r -> p g r u", u=2))
+            groups[b] = grp
+            xc = work.tile([P, MAX_BUNCH * 256], U32, name="xc", tag="xc", align_bytes=64)
+            xs = work.tile([P, MAX_BUNCH * 256], U8, name="xs", tag="xs", align_bytes=64)
+            codes[b] = (xc, xs)
+
+        def pieces(b):
+            size = len(bunches[b])
+            return [(lo, lo + 2) for lo in range(0, size, 2)]
+
+        def quantise(b, piece):
+            lo, hi = piece
+            xc, xs = codes[b]
+            nc.vector.quantize_mx(
+                out=xc[:, lo * 256 : hi * 256].bitcast(FP8X4),
+                scales=xs[:, lo * 256 : hi * 256],
+                in_=groups[b][:, lo * 1024 : hi * 1024],
+            )
+
+        def store(s, j0, j1):
+            nc.sync.dma_start(out=ov[s][:, j0 * D_OUT : j1 * D_OUT], in_=o_tiles[s][:, j0 * D_OUT : j1 * D_OUT])
+
+        def passes(b, i):
+            rt = bunches[b][i]
+            s, j = divmod(rt, J)
+            if j == 0:
+                o_slab = slabs.tile([P, J * D_OUT], F32, name="o_slab", tag="slab")
+                o_tiles[s] = o_slab
+            xc, xs = codes[b]
+            ob = psum.tile([P, D_OUT], F32, name="ob", tag="bank")
+            for g in range(2):
+                m_cols = slice((2 * i + g) * P, (2 * i + g + 1) * P)
+                n_cols = slice(g * D_OUT, (g + 1) * D_OUT)
+                nc.tensor.matmul_mx(
+                    out=ob[:],
+                    lhsT=xc[:, m_cols].bitcast(FP8X4),
+                    lhsT_scale=xs[:, m_cols],
+                    rhs=wc[:, n_cols].bitcast(FP8X4),
+                    rhs_scale=ws[:, n_cols],
+                    start=(g == 0),
+                    stop=(g == 1),
+                )
+            o_cols = o_tiles[s][:, j * D_OUT : (j + 1) * D_OUT]
+            if j % GP_EVERY == 0:
+                nc.scalar.copy(out=o_cols, in_=ob[:])
+                nc.gpsimd.tensor_tensor(out=o_cols, in0=o_cols, in1=bias_sb[:], op=ADD)
+            else:
+                nc.vector.tensor_tensor(out=o_cols, in0=ob[:], in1=bias_sb[:], op=ADD)
+            step = J if s < SLABS - FINE_SLABS else 2
+            if (j + 1) % step == 0:
+                store(s, j + 1 - step, j + 1)
+
+        for t in range(4):
+            weight_bank(0, t, True)
+        weight_quantise(0)
+        transposes(0)
+        weight_bank(1, 0, True)
+        weight_bank(1, 1, True)
+        weight_bank(1, 2, False)
+        weight_bank(1, 3, False)
+        for piece in pieces(0):
+            quantise(0, piece)
+        weight_quantise(1)
+        pb = psum.tile([P, D_OUT], F32, name="pb", tag="bank")
+        nc.tensor.matmul(pb[:], lhsT=ones[:], rhs=bias_row[:], start=True, stop=True)
+        nc.scalar.copy(out=bias_sb[:], in_=pb[:])
+        transposes(1)
+
+        for b in range(len(bunches)):
+            todo = pieces(b + 1) if b + 1 < len(bunches) else []
+            if todo:
+                quantise(b + 1, todo[0])
+            for i in range(len(bunches[b])):
+                passes(b, i)
+                if i + 1 < len(todo):
+                    quantise(b + 1, todo[i + 1])
+            if b + 2 < len(bunches):
+                transposes(b + 2)

@@ -22,7 +22,9 @@ BUNCH_SIZES = [4, 4] + [8] * 7
 MAX_BUNCH = 8
 FINE_SLABS = 2
 WARM_UP = 4
-GP_EVERY = 4
+SORTED_BY_VECTOR = (1,)
+SORTED_BY_SCALAR = (2, 3, 5, 6, 7)
+FIRST_SORTED = 2
 FLOPS = 2 * ROWS * D_IN * D_OUT + 2 * D_OUT * RANK * D_IN
 
 
@@ -32,7 +34,7 @@ def tile_loralinear_t_kernel(tc, x, weight, bias, lora_left, lora_right, out):
     ov = out.flatten_outer_dims().rearrange("(s p j) o -> s p (j o)", p=P, j=J)
     with ExitStack() as ctx:
         const = ctx.enter_context(tc.tile_pool(name="const", bufs=1))
-        slabs = ctx.enter_context(tc.tile_pool(name="slabs", bufs=9))
+        slabs = ctx.enter_context(tc.tile_pool(name="slabs", bufs=8))
         work = ctx.enter_context(tc.tile_pool(name="work", bufs=2))
         psum = ctx.enter_context(tc.psum_pool(name="psum", bufs=8))
         ctx.enter_context(tc.manual_schedule())
@@ -115,6 +117,27 @@ def tile_loralinear_t_kernel(tc, x, weight, bias, lora_left, lora_right, out):
         codes = {}
         o_tiles = {}
 
+        sorted_words = {}
+
+        def sort_words(b):
+            if b < FIRST_SORTED or b >= len(bunches):
+                return
+            srt = work.tile([P, len(SORTED_BY_VECTOR + SORTED_BY_SCALAR) * 512], F32, name="srt", tag="srt")
+            n = 0
+            for rt in bunches[b]:
+                s, j = divmod(rt, J)
+                if j not in SORTED_BY_VECTOR + SORTED_BY_SCALAR:
+                    continue
+                src = x_tiles[s][:].bitcast(F32)[:, j * 512 : (j + 1) * 512].rearrange("p (w u) -> p u w", u=2)
+                words = srt[:, n * 512 : (n + 1) * 512]
+                dst = words.rearrange("p (u w) -> p u w", u=2)
+                if j in SORTED_BY_VECTOR:
+                    nc.vector.tensor_copy(out=dst, in_=src)
+                else:
+                    nc.scalar.copy(out=dst, in_=src)
+                sorted_words[rt] = words
+                n += 1
+
         def transposes(b):
             tiles = bunches[b]
             grp = work.tile([P, MAX_BUNCH * 1024], BF16, name="grp", tag="grp", align_bytes=64)
@@ -125,8 +148,12 @@ def tile_loralinear_t_kernel(tc, x, weight, bias, lora_left, lora_right, out):
                 tb = psum.tile([P, 4, P], F32, name="tb", tag="bank")
                 for c in range(4):
                     g, u = divmod(c, 2)
-                    w0 = j * 512 + g * 256
-                    nc.tensor.transpose(tb[:, c, :], xw[:, w0 + u : w0 + 256 : 2], ident_f[:])
+                    if rt in sorted_words:
+                        words = sorted_words[rt][:, u * 256 + g * P : u * 256 + (g + 1) * P]
+                    else:
+                        w0 = j * 512 + g * 256
+                        words = xw[:, w0 + u : w0 + 256 : 2]
+                    nc.tensor.transpose(tb[:, c, :], words, ident_f[:])
                 nc.scalar.copy(out=gw[:, i], in_=tb[:].rearrange("p (g u) r -> p g r u", u=2))
             groups[b] = grp
             xc = work.tile([P, MAX_BUNCH * 256], U32, name="xc", tag="xc", align_bytes=64)
@@ -170,11 +197,7 @@ def tile_loralinear_t_kernel(tc, x, weight, bias, lora_left, lora_right, out):
                     stop=(g == 1),
                 )
             o_cols = o_tiles[s][:, j * D_OUT : (j + 1) * D_OUT]
-            if j % GP_EVERY == 0:
-                nc.scalar.copy(out=o_cols, in_=ob[:])
-                nc.gpsimd.tensor_tensor(out=o_cols, in0=o_cols, in1=bias_sb[:], op=ADD)
-            else:
-                nc.vector.tensor_tensor(out=o_cols, in0=ob[:], in1=bias_sb[:], op=ADD)
+            nc.vector.tensor_tensor(out=o_cols, in0=ob[:], in1=bias_sb[:], op=ADD)
             step = J if s < SLABS - FINE_SLABS else 2
             if (j + 1) % step == 0:
                 store(s, j + 1 - step, j + 1)
@@ -194,6 +217,7 @@ def tile_loralinear_t_kernel(tc, x, weight, bias, lora_left, lora_right, out):
         nc.tensor.matmul(pb[:], lhsT=ones[:], rhs=bias_row[:], start=True, stop=True)
         nc.scalar.copy(out=bias_sb[:], in_=pb[:])
         transposes(1)
+        sort_words(2)
 
         for b in range(len(bunches)):
             todo = pieces(b + 1) if b + 1 < len(bunches) else []
@@ -205,3 +229,4 @@ def tile_loralinear_t_kernel(tc, x, weight, bias, lora_left, lora_right, out):
                     quantise(b + 1, todo[i + 1])
             if b + 2 < len(bunches):
                 transposes(b + 2)
+                sort_words(b + 3)

@@ -20,10 +20,11 @@ J = 8
 SLABS = ROWS // (P * J)
 BUNCH_SIZES = [4, 4] + [8] * 7
 MAX_BUNCH = 8
+FINE_LOADS = 2
 FINE_SLABS = 2
 WARM_UP = 4
-SORTED_BY_VECTOR = (1,)
-SORTED_BY_SCALAR = (2, 3, 5, 6, 7)
+SORTED_BY_GPSIMD = (3, 7)
+SORTED_BY_VECTOR = (0,)
 FIRST_SORTED = 2
 FLOPS = 2 * ROWS * D_IN * D_OUT + 2 * D_OUT * RANK * D_IN
 
@@ -57,21 +58,19 @@ def tile_loralinear_t_kernel(tc, x, weight, bias, lora_left, lora_right, out):
         nc.sync.dma_start(out=ll_sb[:], in_=lora_left.rearrange("(t p) r -> p t r", p=P))
         lr_sb = const.tile([P, D_IN], BF16, name="lr_sb")
         nc.sync.dma_start(out=lr_sb[:], in_=lora_right)
+        w_sb = const.tile([P, 4, D_IN], BF16, name="w_sb")
+        w_dram = weight.rearrange("(t p) k -> p t k", p=P)
+        for t in range(4):
+            nc.sync.dma_start(out=w_sb[:, t], in_=w_dram[:, t])
         nc.sync.dma_start(out=bias_row[0:1, :], in_=bias.unsqueeze(0))
-        w_sb = const.tile([P, 2, 4, 512], BF16, name="w_sb")
-        w_dram = weight.rearrange("(t p) (g k) -> g p t k", p=P, g=2)
         x_tiles = []
         for s in range(SLABS):
             x_slab = slabs.tile([P, J * D_IN], BF16, name="x_slab", tag="slab")
             x_tiles.append(x_slab)
-        half = J * D_IN // 2
-        for t in range(4):
-            nc.sync.dma_start(out=w_sb[:, 0, t], in_=w_dram[0][:, t])
-        nc.sync.dma_start(out=x_tiles[0][:, 0:half], in_=xv[0][:, 0:half])
-        nc.sync.dma_start(out=w_sb[:, 1], in_=w_dram[1])
-        nc.sync.dma_start(out=x_tiles[0][:, half : 2 * half], in_=xv[0][:, half : 2 * half])
-        for s in range(1, SLABS):
-            nc.sync.dma_start(out=x_tiles[s][:], in_=xv[s])
+            pieces_of_slab = 2 if s < FINE_LOADS else 1
+            width = J * D_IN // pieces_of_slab
+            for n in range(pieces_of_slab):
+                nc.sync.dma_start(out=x_slab[:, n * width : (n + 1) * width], in_=xv[s][:, n * width : (n + 1) * width])
 
         pl = psum.tile([P, 4, P], BF16, name="pl", tag="bank")
         for t in range(4):
@@ -81,7 +80,7 @@ def tile_loralinear_t_kernel(tc, x, weight, bias, lora_left, lora_right, out):
 
         bias_sb = const.tile([P, D_OUT], F32, name="bias_sb")
 
-        w_view = w_sb[:].rearrange("p g t (q v) -> p g t q v", q=P, v=4)
+        w_view = w_sb[:].rearrange("p t (g q v) -> p t g q v", g=2, q=P, v=4)
         lr_view = lr_sb[:].rearrange("p (g q v) -> p g q v", g=2, q=P, v=4)
         wg = const.tile([P, 2, D_OUT, 4], BF16, name="wg", align_bytes=64)
         wc = const.tile([P, 2 * D_OUT], U32, name="wc", align_bytes=64)
@@ -90,7 +89,7 @@ def tile_loralinear_t_kernel(tc, x, weight, bias, lora_left, lora_right, out):
         def weight_bank(g, t, on_vector):
             pw = psum.tile([P, 4, P], F32, name="pw", tag="bank")
             for v in range(4):
-                nc.tensor.matmul(pw[:, v, :], lhsT=w_view[:, g, t, :, v], rhs=ident_bf[:], start=True, stop=False)
+                nc.tensor.matmul(pw[:, v, :], lhsT=w_view[:, t, g, :, v], rhs=ident_bf[:], start=True, stop=False)
                 nc.tensor.matmul(
                     pw[:, v, :], lhsT=lr_view[:, g, :, v], rhs=ll_t2[:, t * P : (t + 1) * P], start=False, stop=True
                 )
@@ -117,30 +116,31 @@ def tile_loralinear_t_kernel(tc, x, weight, bias, lora_left, lora_right, out):
         codes = {}
         o_tiles = {}
 
-        sorted_words = {}
+        def group_tile(b):
+            grp = groups.get(b)
+            if grp is None:
+                grp = work.tile([P, MAX_BUNCH * 1024], BF16, name="grp", tag="grp", bufs=3, align_bytes=64)
+                groups[b] = grp
+            return grp
 
         def sort_words(b):
             if b < FIRST_SORTED or b >= len(bunches):
                 return
-            srt = work.tile([P, len(SORTED_BY_VECTOR + SORTED_BY_SCALAR) * 512], F32, name="srt", tag="srt")
-            n = 0
-            for rt in bunches[b]:
+            grp = group_tile(b)
+            for i, rt in enumerate(bunches[b]):
                 s, j = divmod(rt, J)
-                if j not in SORTED_BY_VECTOR + SORTED_BY_SCALAR:
-                    continue
                 src = x_tiles[s][:].bitcast(F32)[:, j * 512 : (j + 1) * 512].rearrange("p (w u) -> p u w", u=2)
-                words = srt[:, n * 512 : (n + 1) * 512]
-                dst = words.rearrange("p (u w) -> p u w", u=2)
-                if j in SORTED_BY_VECTOR:
+                dst = grp[:].bitcast(F32)[:, i * 512 : (i + 1) * 512].rearrange("p (u w) -> p u w", u=2)
+                if j in SORTED_BY_GPSIMD:
+                    nc.gpsimd.tensor_copy(out=dst, in_=src)
+                elif j in SORTED_BY_VECTOR:
                     nc.vector.tensor_copy(out=dst, in_=src)
                 else:
                     nc.scalar.copy(out=dst, in_=src)
-                sorted_words[rt] = words
-                n += 1
 
         def transposes(b):
             tiles = bunches[b]
-            grp = work.tile([P, MAX_BUNCH * 1024], BF16, name="grp", tag="grp", align_bytes=64)
+            grp = group_tile(b)
             gw = grp[:].bitcast(F32).rearrange("p (i g r u) -> p i g r u", i=MAX_BUNCH, g=2, r=P, u=2)
             for i, rt in enumerate(tiles):
                 s, j = divmod(rt, J)
@@ -148,14 +148,14 @@ def tile_loralinear_t_kernel(tc, x, weight, bias, lora_left, lora_right, out):
                 tb = psum.tile([P, 4, P], F32, name="tb", tag="bank")
                 for c in range(4):
                     g, u = divmod(c, 2)
-                    if rt in sorted_words:
-                        words = sorted_words[rt][:, u * 256 + g * P : u * 256 + (g + 1) * P]
+                    if b >= FIRST_SORTED:
+                        w0 = i * 512 + u * 256 + g * P
+                        words = grp[:].bitcast(F32)[:, w0 : w0 + P]
                     else:
                         w0 = j * 512 + g * 256
                         words = xw[:, w0 + u : w0 + 256 : 2]
                     nc.tensor.transpose(tb[:, c, :], words, ident_f[:])
                 nc.scalar.copy(out=gw[:, i], in_=tb[:].rearrange("p (g u) r -> p g r u", u=2))
-            groups[b] = grp
             xc = work.tile([P, MAX_BUNCH * 256], U32, name="xc", tag="xc", align_bytes=64)
             xs = work.tile([P, MAX_BUNCH * 256], U8, name="xs", tag="xs", align_bytes=64)
             codes[b] = (xc, xs)
@@ -204,15 +204,12 @@ def tile_loralinear_t_kernel(tc, x, weight, bias, lora_left, lora_right, out):
 
         for t in range(4):
             weight_bank(0, t, True)
-        weight_quantise(0)
+            weight_bank(1, t, False)
         transposes(0)
-        weight_bank(1, 0, True)
-        weight_bank(1, 1, True)
-        weight_bank(1, 2, False)
-        weight_bank(1, 3, False)
+        weight_quantise(0)
+        weight_quantise(1)
         for piece in pieces(0):
             quantise(0, piece)
-        weight_quantise(1)
         pb = psum.tile([P, D_OUT], F32, name="pb", tag="bank")
         nc.tensor.matmul(pb[:], lhsT=ones[:], rhs=bias_row[:], start=True, stop=True)
         nc.scalar.copy(out=bias_sb[:], in_=pb[:])

@@ -16,6 +16,7 @@ D_IN = 1024
 D_OUT = 512
 RANK = 128
 LORA_SCALE = 2.0
+BANKS = 8
 J = 8
 SLABS = ROWS // (P * J)
 BUNCH_SIZES = [4, 4] + [8] * 7
@@ -35,10 +36,17 @@ def tile_loralinear_t_kernel(tc, x, weight, bias, lora_left, lora_right, out):
     ov = out.flatten_outer_dims().rearrange("(s p j) o -> s p (j o)", p=P, j=J)
     with ExitStack() as ctx:
         const = ctx.enter_context(tc.tile_pool(name="const", bufs=1))
-        slabs = ctx.enter_context(tc.tile_pool(name="slabs", bufs=8))
-        work = ctx.enter_context(tc.tile_pool(name="work", bufs=2))
-        psum = ctx.enter_context(tc.psum_pool(name="psum", bufs=8))
+        slabs = ctx.enter_context(tc.tile_pool(name="slabs", bufs=1))
+        work = ctx.enter_context(tc.tile_pool(name="work", bufs=1))
+        psum = ctx.enter_context(tc.psum_pool(name="psum", bufs=1))
         ctx.enter_context(tc.manual_schedule())
+        taken = []
+
+        def bank(shape, dtype):
+            tag = "bank%d" % (len(taken) % BANKS)
+            tile = psum.tile(shape, dtype, name=tag, tag=tag)
+            taken.append(tag)
+            return tile
 
         ident_bf = const.tile([P, P], BF16, name="ident_bf")
         masks.make_identity(nc, ident_bf[:])
@@ -50,7 +58,7 @@ def tile_loralinear_t_kernel(tc, x, weight, bias, lora_left, lora_right, out):
         nc.vector.memset(warm[:], 0.0)
         bias_row = const.tile([P, D_OUT], BF16, name="bias_row")
         nc.vector.memset(bias_row[:], 0.0)
-        pd = psum.tile([P, D_OUT], F32, name="pd", tag="bank")
+        pd = bank([P, D_OUT], F32)
         for n in range(WARM_UP):
             nc.tensor.matmul(pd[:], lhsT=ones[:], rhs=warm[:], start=True, stop=True)
 
@@ -65,14 +73,14 @@ def tile_loralinear_t_kernel(tc, x, weight, bias, lora_left, lora_right, out):
         nc.sync.dma_start(out=bias_row[0:1, :], in_=bias.unsqueeze(0))
         x_tiles = []
         for s in range(SLABS):
-            x_slab = slabs.tile([P, J * D_IN], BF16, name="x_slab", tag="slab")
+            x_slab = slabs.tile([P, J * D_IN], BF16, name="x_slab", tag="slab%d" % s)
             x_tiles.append(x_slab)
             pieces_of_slab = 2 if s < FINE_LOADS else 1
             width = J * D_IN // pieces_of_slab
             for n in range(pieces_of_slab):
                 nc.sync.dma_start(out=x_slab[:, n * width : (n + 1) * width], in_=xv[s][:, n * width : (n + 1) * width])
 
-        pl = psum.tile([P, 4, P], BF16, name="pl", tag="bank")
+        pl = bank([P, 4, P], BF16)
         for t in range(4):
             nc.tensor.transpose(pl[:, t, :], ll_sb[:, t, :], ident_bf[:])
         ll_t2 = const.tile([P, D_OUT], BF16, name="ll_t2")
@@ -87,7 +95,7 @@ def tile_loralinear_t_kernel(tc, x, weight, bias, lora_left, lora_right, out):
         ws = const.tile([P, 2 * D_OUT], U8, name="ws", align_bytes=64)
 
         def weight_bank(g, t, on_vector):
-            pw = psum.tile([P, 4, P], F32, name="pw", tag="bank")
+            pw = bank([P, 4, P], F32)
             for v in range(4):
                 nc.tensor.matmul(pw[:, v, :], lhsT=w_view[:, t, g, :, v], rhs=ident_bf[:], start=True, stop=False)
                 nc.tensor.matmul(
@@ -119,7 +127,7 @@ def tile_loralinear_t_kernel(tc, x, weight, bias, lora_left, lora_right, out):
         def group_tile(b):
             grp = groups.get(b)
             if grp is None:
-                grp = work.tile([P, MAX_BUNCH * 1024], BF16, name="grp", tag="grp", bufs=3, align_bytes=64)
+                grp = work.tile([P, MAX_BUNCH * 1024], BF16, name="grp", tag="grp%d" % (b % 3), align_bytes=64)
                 groups[b] = grp
             return grp
 
@@ -145,7 +153,7 @@ def tile_loralinear_t_kernel(tc, x, weight, bias, lora_left, lora_right, out):
             for i, rt in enumerate(tiles):
                 s, j = divmod(rt, J)
                 xw = x_tiles[s][:].bitcast(F32)
-                tb = psum.tile([P, 4, P], F32, name="tb", tag="bank")
+                tb = bank([P, 4, P], F32)
                 for c in range(4):
                     g, u = divmod(c, 2)
                     if b >= FIRST_SORTED:
@@ -156,8 +164,8 @@ def tile_loralinear_t_kernel(tc, x, weight, bias, lora_left, lora_right, out):
                         words = xw[:, w0 + u : w0 + 256 : 2]
                     nc.tensor.transpose(tb[:, c, :], words, ident_f[:])
                 nc.scalar.copy(out=gw[:, i], in_=tb[:].rearrange("p (g u) r -> p g r u", u=2))
-            xc = work.tile([P, MAX_BUNCH * 256], U32, name="xc", tag="xc", align_bytes=64)
-            xs = work.tile([P, MAX_BUNCH * 256], U8, name="xs", tag="xs", align_bytes=64)
+            xc = work.tile([P, MAX_BUNCH * 256], U32, name="xc", tag="xc%d" % (b % 2), align_bytes=64)
+            xs = work.tile([P, MAX_BUNCH * 256], U8, name="xs", tag="xs%d" % (b % 2), align_bytes=64)
             codes[b] = (xc, xs)
 
         def pieces(b):
@@ -180,10 +188,10 @@ def tile_loralinear_t_kernel(tc, x, weight, bias, lora_left, lora_right, out):
             rt = bunches[b][i]
             s, j = divmod(rt, J)
             if j == 0:
-                o_slab = slabs.tile([P, J * D_OUT], F32, name="o_slab", tag="slab")
+                o_slab = slabs.tile([P, J * D_OUT], F32, name="o_slab", tag="slab%d" % s)
                 o_tiles[s] = o_slab
             xc, xs = codes[b]
-            ob = psum.tile([P, D_OUT], F32, name="ob", tag="bank")
+            ob = bank([P, D_OUT], F32)
             for g in range(2):
                 m_cols = slice((2 * i + g) * P, (2 * i + g + 1) * P)
                 n_cols = slice(g * D_OUT, (g + 1) * D_OUT)
@@ -210,7 +218,7 @@ def tile_loralinear_t_kernel(tc, x, weight, bias, lora_left, lora_right, out):
         weight_quantise(1)
         for piece in pieces(0):
             quantise(0, piece)
-        pb = psum.tile([P, D_OUT], F32, name="pb", tag="bank")
+        pb = bank([P, D_OUT], F32)
         nc.tensor.matmul(pb[:], lhsT=ones[:], rhs=bias_row[:], start=True, stop=True)
         nc.scalar.copy(out=bias_sb[:], in_=pb[:])
         transposes(1)
@@ -218,12 +226,15 @@ def tile_loralinear_t_kernel(tc, x, weight, bias, lora_left, lora_right, out):
 
         for b in range(len(bunches)):
             todo = pieces(b + 1) if b + 1 < len(bunches) else []
-            if todo:
-                quantise(b + 1, todo[0])
-            for i in range(len(bunches[b])):
-                passes(b, i)
-                if i + 1 < len(todo):
-                    quantise(b + 1, todo[i + 1])
             if b + 2 < len(bunches):
+                for i in range(len(bunches[b])):
+                    passes(b, i)
+                for piece in todo:
+                    quantise(b + 1, piece)
                 transposes(b + 2)
                 sort_words(b + 3)
+            else:
+                for i in range(len(bunches[b])):
+                    if i < len(todo):
+                        quantise(b + 1, todo[i])
+                    passes(b, i)

@@ -21,11 +21,12 @@ J = 8
 SLABS = ROWS // (P * J)
 BUNCH_SIZES = [4, 4] + [8] * 7
 MAX_BUNCH = 8
-FINE_LOADS = 2
+FINE_LOADS = 4
 FINE_SLABS = 2
 WARM_UP = 4
-SORTED_BY_GPSIMD = (3, 7)
-SORTED_BY_VECTOR = (0,)
+EARLY_SORTERS = "VGVGSGSG"
+SORTERS = "VSSGSSSG"
+EARLY = 3
 FIRST_SORTED = 2
 FLOPS = 2 * ROWS * D_IN * D_OUT + 2 * D_OUT * RANK * D_IN
 
@@ -139,9 +140,10 @@ def tile_loralinear_t_kernel(tc, x, weight, bias, lora_left, lora_right, out):
                 s, j = divmod(rt, J)
                 src = x_tiles[s][:].bitcast(F32)[:, j * 512 : (j + 1) * 512].rearrange("p (w u) -> p u w", u=2)
                 dst = grp[:].bitcast(F32)[:, i * 512 : (i + 1) * 512].rearrange("p (u w) -> p u w", u=2)
-                if j in SORTED_BY_GPSIMD:
+                sorter = (EARLY_SORTERS if b <= EARLY else SORTERS)[j]
+                if sorter == "G":
                     nc.gpsimd.tensor_copy(out=dst, in_=src)
-                elif j in SORTED_BY_VECTOR:
+                elif sorter == "V":
                     nc.vector.tensor_copy(out=dst, in_=src)
                 else:
                     nc.scalar.copy(out=dst, in_=src)
@@ -206,7 +208,7 @@ def tile_loralinear_t_kernel(tc, x, weight, bias, lora_left, lora_right, out):
                 )
             o_cols = o_tiles[s][:, j * D_OUT : (j + 1) * D_OUT]
             nc.vector.tensor_tensor(out=o_cols, in0=ob[:], in1=bias_sb[:], op=ADD)
-            step = J if s < SLABS - FINE_SLABS else 2
+            step = 4 if s < SLABS - FINE_SLABS else 2
             if (j + 1) % step == 0:
                 store(s, j + 1 - step, j + 1)
 

@@ -24,10 +24,10 @@ MAX_BUNCH = 8
 FINE_LOADS = 4
 FINE_SLABS = 2
 WARM_UP = 4
+HEAD_SORTERS = "--VG--VG"
 EARLY_SORTERS = "VGVGSGSG"
 SORTERS = "VSSGSSSG"
 EARLY = 3
-FIRST_SORTED = 2
 FLOPS = 2 * ROWS * D_IN * D_OUT + 2 * D_OUT * RANK * D_IN
 
 
@@ -89,31 +89,49 @@ def tile_loralinear_t_kernel(tc, x, weight, bias, lora_left, lora_right, out):
 
         bias_sb = const.tile([P, D_OUT], F32, name="bias_sb")
 
-        w_view = w_sb[:].rearrange("p t (g q v) -> p t g q v", g=2, q=P, v=4)
-        lr_view = lr_sb[:].rearrange("p (g q v) -> p g q v", g=2, q=P, v=4)
-        wg = const.tile([P, 2, D_OUT, 4], BF16, name="wg", align_bytes=64)
+        we_sb = const.tile([P, 4, D_IN], BF16, name="we_sb")
+        wg = []
+        for g in range(2):
+            wg_g = const.tile([P, D_OUT, 4], BF16, name="wg_g", tag="wg%d" % g, align_bytes=64)
+            wg.append(wg_g)
         wc = const.tile([P, 2 * D_OUT], U32, name="wc", align_bytes=64)
         ws = const.tile([P, 2 * D_OUT], U8, name="ws", align_bytes=64)
-
-        def weight_bank(g, t, on_vector):
-            pw = bank([P, 4, P], F32)
-            for v in range(4):
-                nc.tensor.matmul(pw[:, v, :], lhsT=w_view[:, t, g, :, v], rhs=ident_bf[:], start=True, stop=False)
+        for t in range(4):
+            for g in range(2):
+                pw = bank([P, 512], F32)
                 nc.tensor.matmul(
-                    pw[:, v, :], lhsT=lr_view[:, g, :, v], rhs=ll_t2[:, t * P : (t + 1) * P], start=False, stop=True
+                    pw[:], lhsT=ll_t2[:, t * P : (t + 1) * P], rhs=lr_sb[:, g * 512 : (g + 1) * 512], start=True, stop=True
                 )
-            dst = wg[:, g, t * P : (t + 1) * P, :]
-            src = pw[:].rearrange("p v o -> p o v")
-            if on_vector:
-                nc.vector.tensor_copy(out=dst, in_=src)
-            else:
-                nc.scalar.copy(out=dst, in_=src)
+                nc.vector.tensor_tensor(
+                    out=we_sb[:, t].rearrange("p (u g q e) -> p g u q e", u=2, g=2, e=2)[:, g],
+                    in0=pw[:].rearrange("p (q u e) -> p u q e", u=2, e=2),
+                    in1=w_sb[:, t, g * 512 : (g + 1) * 512].rearrange("p (q u e) -> p u q e", u=2, e=2),
+                    op=ADD,
+                )
 
-        def weight_quantise(g):
-            cols = slice(g * D_OUT, (g + 1) * D_OUT)
-            nc.vector.quantize_mx(
-                out=wc[:, cols].bitcast(FP8X4), scales=ws[:, cols], in_=wg[:, g].rearrange("p o v -> p (o v)")
-            )
+        def weight_transposes(t):
+            tb = bank([P, 4, P], F32)
+            words = we_sb[:, t].bitcast(F32)
+            for c in range(4):
+                g, u = divmod(c, 2)
+                w0 = u * 256 + g * P
+                nc.tensor.transpose(tb[:, c, :], words[:, w0 : w0 + P], ident_f[:])
+            for g in range(2):
+                dst = wg[g][:, t * P : (t + 1) * P, :].rearrange("p o v -> p (o v)").bitcast(F32)
+                nc.scalar.copy(
+                    out=dst.rearrange("p (o u) -> p o u", u=2),
+                    in_=tb[:, 2 * g : 2 * g + 2, :].rearrange("p u o -> p o u"),
+                )
+
+        def weight_quantise(half):
+            for g in range(2):
+                o_cols = slice(half * 256, (half + 1) * 256)
+                cols = slice(g * D_OUT + half * 256, g * D_OUT + (half + 1) * 256)
+                nc.vector.quantize_mx(
+                    out=wc[:, cols].bitcast(FP8X4),
+                    scales=ws[:, cols],
+                    in_=wg[g][:, o_cols].rearrange("p o v -> p (o v)"),
+                )
 
         bunches = []
         first = 0
@@ -132,15 +150,22 @@ def tile_loralinear_t_kernel(tc, x, weight, bias, lora_left, lora_right, out):
                 groups[b] = grp
             return grp
 
+        def sorter_of(b, j):
+            if b < 2:
+                return HEAD_SORTERS[j]
+            return (EARLY_SORTERS if b <= EARLY else SORTERS)[j]
+
         def sort_words(b):
-            if b < FIRST_SORTED or b >= len(bunches):
+            if b >= len(bunches):
                 return
             grp = group_tile(b)
             for i, rt in enumerate(bunches[b]):
                 s, j = divmod(rt, J)
+                sorter = sorter_of(b, j)
+                if sorter == "-":
+                    continue
                 src = x_tiles[s][:].bitcast(F32)[:, j * 512 : (j + 1) * 512].rearrange("p (w u) -> p u w", u=2)
                 dst = grp[:].bitcast(F32)[:, i * 512 : (i + 1) * 512].rearrange("p (u w) -> p u w", u=2)
-                sorter = (EARLY_SORTERS if b <= EARLY else SORTERS)[j]
                 if sorter == "G":
                     nc.gpsimd.tensor_copy(out=dst, in_=src)
                 elif sorter == "V":
@@ -158,7 +183,7 @@ def tile_loralinear_t_kernel(tc, x, weight, bias, lora_left, lora_right, out):
                 tb = bank([P, 4, P], F32)
                 for c in range(4):
                     g, u = divmod(c, 2)
-                    if b >= FIRST_SORTED:
+                    if sorter_of(b, j) != "-":
                         w0 = i * 512 + u * 256 + g * P
                         words = grp[:].bitcast(F32)[:, w0 : w0 + P]
                     else:
@@ -213,11 +238,12 @@ def tile_loralinear_t_kernel(tc, x, weight, bias, lora_left, lora_right, out):
                 store(s, j + 1 - step, j + 1)
 
         for t in range(4):
-            weight_bank(0, t, True)
-            weight_bank(1, t, False)
+            weight_transposes(t)
+        sort_words(0)
         transposes(0)
         weight_quantise(0)
         weight_quantise(1)
+        sort_words(1)
         for piece in pieces(0):
             quantise(0, piece)
         pb = bank([P, D_OUT], F32)

@@ -21,8 +21,8 @@ J = 8
 SLABS = ROWS // (P * J)
 BUNCH_SIZES = [4, 4] + [8] * 7
 MAX_BUNCH = 8
-FINE_LOADS = 4
-FINE_SLABS = 2
+FINE_LOADS = 3
+STORE_STEPS = [8] * 5 + [4, 4, 2]
 WARM_UP = 4
 HEAD_SORTERS = "--VG--VG"
 EARLY_SORTERS = "VGVGSGSG"
@@ -69,8 +69,8 @@ def tile_loralinear_t_kernel(tc, x, weight, bias, lora_left, lora_right, out):
         nc.sync.dma_start(out=lr_sb[:], in_=lora_right)
         w_sb = const.tile([P, 4, D_IN], BF16, name="w_sb")
         w_dram = weight.rearrange("(t p) k -> p t k", p=P)
-        for t in range(4):
-            nc.sync.dma_start(out=w_sb[:, t], in_=w_dram[:, t])
+        for t in range(0, 4, 2):
+            nc.sync.dma_start(out=w_sb[:, t : t + 2], in_=w_dram[:, t : t + 2])
         nc.sync.dma_start(out=bias_row[0:1, :], in_=bias.unsqueeze(0))
         x_tiles = []
         for s in range(SLABS):
@@ -233,7 +233,7 @@ def tile_loralinear_t_kernel(tc, x, weight, bias, lora_left, lora_right, out):
                 )
             o_cols = o_tiles[s][:, j * D_OUT : (j + 1) * D_OUT]
             nc.vector.tensor_tensor(out=o_cols, in0=ob[:], in1=bias_sb[:], op=ADD)
-            step = 4 if s < SLABS - FINE_SLABS else 2
+            step = STORE_STEPS[s]
             if (j + 1) % step == 0:
                 store(s, j + 1 - step, j + 1)
 

from contextlib import ExitStack

import concourse.masks as masks
import concourse.mybir as mybir

F32 = mybir.dt.float32
BF16 = mybir.dt.bfloat16
U32 = mybir.dt.uint32
U8 = mybir.dt.uint8
FP8X4 = mybir.dt.float8_e4m3fn_x4
ADD = mybir.AluOpType.add

P = 128
ROWS = 8192
D_IN = 1024
D_OUT = 512
RANK = 128
LORA_SCALE = 2.0
BANKS = 8
J = 8
SLABS = ROWS // (P * J)
BUNCH_SIZES = [4, 4] + [8] * 7
MAX_BUNCH = 8
FINE_LOADS = 3
STORE_STEPS = [8] * 5 + [4, 4, 2]
WARM_UP = 4
HEAD_SORTERS = "--VG--VG"
EARLY_SORTERS = "VGVGSGSG"
SORTERS = "VSSGSSSG"
EARLY = 3
FLOPS = 2 * ROWS * D_IN * D_OUT + 2 * D_OUT * RANK * D_IN


def tile_loralinear_t_kernel(tc, x, weight, bias, lora_left, lora_right, out):
    nc = tc.nc
    xv = x.flatten_outer_dims().rearrange("(s p j) k -> s p (j k)", p=P, j=J)
    ov = out.flatten_outer_dims().rearrange("(s p j) o -> s p (j o)", p=P, j=J)
    with ExitStack() as ctx:
        const = ctx.enter_context(tc.tile_pool(name="const", bufs=1))
        slabs = ctx.enter_context(tc.tile_pool(name="slabs", bufs=1))
        work = ctx.enter_context(tc.tile_pool(name="work", bufs=1))
        psum = ctx.enter_context(tc.psum_pool(name="psum", bufs=1))
        ctx.enter_context(tc.manual_schedule())
        taken = []

        def bank(shape, dtype):
            tag = "bank%d" % (len(taken) % BANKS)
            tile = psum.tile(shape, dtype, name=tag, tag=tag)
            taken.append(tag)
            return tile

        ident_bf = const.tile([P, P], BF16, name="ident_bf")
        masks.make_identity(nc, ident_bf[:])
        ident_f = const.tile([P, P], F32, name="ident_f")
        masks.make_identity(nc, ident_f[:])
        ones = const.tile([P, P], BF16, name="ones")
        nc.vector.memset(ones[:], 1.0)
        warm = const.tile([P, D_OUT], BF16, name="warm")
        nc.vector.memset(warm[:], 0.0)
        bias_row = const.tile([P, D_OUT], BF16, name="bias_row")
        nc.vector.memset(bias_row[:], 0.0)
        pd = bank([P, D_OUT], F32)
        for n in range(WARM_UP):
            nc.tensor.matmul(pd[:], lhsT=ones[:], rhs=warm[:], start=True, stop=True)

        ll_sb = const.tile([P, 4, RANK], BF16, name="ll_sb")
        nc.sync.dma_start(out=ll_sb[:], in_=lora_left.rearrange("(t p) r -> p t r", p=P))
        lr_sb = const.tile([P, D_IN], BF16, name="lr_sb")
        nc.sync.dma_start(out=lr_sb[:], in_=lora_right)
        w_sb = const.tile([P, 4, D_IN], BF16, name="w_sb")
        w_dram = weight.rearrange("(t p) k -> p t k", p=P)
        for t in range(0, 4, 2):
            nc.sync.dma_start(out=w_sb[:, t : t + 2], in_=w_dram[:, t : t + 2])
        nc.sync.dma_start(out=bias_row[0:1, :], in_=bias.unsqueeze(0))
        x_tiles = []
        for s in range(SLABS):
            x_slab = slabs.tile([P, J * D_IN], BF16, name="x_slab", tag="slab%d" % s)
            x_tiles.append(x_slab)
            pieces_of_slab = 2 if s < FINE_LOADS else 1
            width = J * D_IN // pieces_of_slab
            for n in range(pieces_of_slab):
                nc.sync.dma_start(out=x_slab[:, n * width : (n + 1) * width], in_=xv[s][:, n * width : (n + 1) * width])

        pl = bank([P, 4, P], BF16)
        for t in range(4):
            nc.tensor.transpose(pl[:, t, :], ll_sb[:, t, :], ident_bf[:])
        ll_t2 = const.tile([P, D_OUT], BF16, name="ll_t2")
        nc.vector.tensor_scalar_mul(out=ll_t2[:], in0=pl[:].rearrange("p t o -> p (t o)"), scalar1=LORA_SCALE)

        bias_sb = const.tile([P, D_OUT], F32, name="bias_sb")

        we_sb = const.tile([P, 4, D_IN], BF16, name="we_sb")
        wg = []
        for g in range(2):
            wg_g = const.tile([P, D_OUT, 4], BF16, name="wg_g", tag="wg%d" % g, align_bytes=64)
            wg.append(wg_g)
        wc = const.tile([P, 2 * D_OUT], U32, name="wc", align_bytes=64)
        ws = const.tile([P, 2 * D_OUT], U8, name="ws", align_bytes=64)
        for t in range(4):
            for g in range(2):
                pw = bank([P, 512], F32)
                nc.tensor.matmul(
                    pw[:], lhsT=ll_t2[:, t * P : (t + 1) * P], rhs=lr_sb[:, g * 512 : (g + 1) * 512], start=True, stop=True
                )
                nc.vector.tensor_tensor(
                    out=we_sb[:, t].rearrange("p (u g q e) -> p g u q e", u=2, g=2, e=2)[:, g],
                    in0=pw[:].rearrange("p (q u e) -> p u q e", u=2, e=2),
                    in1=w_sb[:, t, g * 512 : (g + 1) * 512].rearrange("p (q u e) -> p u q e", u=2, e=2),
                    op=ADD,
                )

        def weight_transposes(t):
            tb = bank([P, 4, P], F32)
            words = we_sb[:, t].bitcast(F32)
            for c in range(4):
                g, u = divmod(c, 2)
                w0 = u * 256 + g * P
                nc.tensor.transpose(tb[:, c, :], words[:, w0 : w0 + P], ident_f[:])
            for g in range(2):
                dst = wg[g][:, t * P : (t + 1) * P, :].rearrange("p o v -> p (o v)").bitcast(F32)
                nc.scalar.copy(
                    out=dst.rearrange("p (o u) -> p o u", u=2),
                    in_=tb[:, 2 * g : 2 * g + 2, :].rearrange("p u o -> p o u"),
                )

        def weight_quantise(half):
            for g in range(2):
                o_cols = slice(half * 256, (half + 1) * 256)
                cols = slice(g * D_OUT + half * 256, g * D_OUT + (half + 1) * 256)
                nc.vector.quantize_mx(
                    out=wc[:, cols].bitcast(FP8X4),
                    scales=ws[:, cols],
                    in_=wg[g][:, o_cols].rearrange("p o v -> p (o v)"),
                )

        bunches = []
        first = 0
        for size in BUNCH_SIZES:
            bunches.append(list(range(first, first + size)))
            first += size
        assert first == ROWS // P
        groups = {}
        codes = {}
        o_tiles = {}

        def group_tile(b):
            grp = groups.get(b)
            if grp is None:
                grp = work.tile([P, MAX_BUNCH * 1024], BF16, name="grp", tag="grp%d" % (b % 3), align_bytes=64)
                groups[b] = grp
            return grp

        def sorter_of(b, j):
            if b < 2:
                return HEAD_SORTERS[j]
            return (EARLY_SORTERS if b <= EARLY else SORTERS)[j]

        def sort_words(b):
            if b >= len(bunches):
                return
            grp = group_tile(b)
            for i, rt in enumerate(bunches[b]):
                s, j = divmod(rt, J)
                sorter = sorter_of(b, j)
                if sorter == "-":
                    continue
                src = x_tiles[s][:].bitcast(F32)[:, j * 512 : (j + 1) * 512].rearrange("p (w u) -> p u w", u=2)
                dst = grp[:].bitcast(F32)[:, i * 512 : (i + 1) * 512].rearrange("p (u w) -> p u w", u=2)
                if sorter == "G":
                    nc.gpsimd.tensor_copy(out=dst, in_=src)
                elif sorter == "V":
                    nc.vector.tensor_copy(out=dst, in_=src)
                else:
                    nc.scalar.copy(out=dst, in_=src)

        def transposes(b):
            tiles = bunches[b]
            grp = group_tile(b)
            gw = grp[:].bitcast(F32).rearrange("p (i g r u) -> p i g r u", i=MAX_BUNCH, g=2, r=P, u=2)
            for i, rt in enumerate(tiles):
                s, j = divmod(rt, J)
                xw = x_tiles[s][:].bitcast(F32)
                tb = bank([P, 4, P], F32)
                for c in range(4):
                    g, u = divmod(c, 2)
                    if sorter_of(b, j) != "-":
                        w0 = i * 512 + u * 256 + g * P
                        words = grp[:].bitcast(F32)[:, w0 : w0 + P]
                    else:
                        w0 = j * 512 + g * 256
                        words = xw[:, w0 + u : w0 + 256 : 2]
                    nc.tensor.transpose(tb[:, c, :], words, ident_f[:])
                nc.scalar.copy(out=gw[:, i], in_=tb[:].rearrange("p (g u) r -> p g r u", u=2))
            xc = work.tile([P, MAX_BUNCH * 256], U32, name="xc", tag="xc%d" % (b % 2), align_bytes=64)
            xs = work.tile([P, MAX_BUNCH * 256], U8, name="xs", tag="xs%d" % (b % 2), align_bytes=64)
            codes[b] = (xc, xs)

        def pieces(b):
            size = len(bunches[b])
            return [(lo, lo + 2) for lo in range(0, size, 2)]

        def quantise(b, piece):
            lo, hi = piece
            xc, xs = codes[b]
            nc.vector.quantize_mx(
                out=xc[:, lo * 256 : hi * 256].bitcast(FP8X4),
                scales=xs[:, lo * 256 : hi * 256],
                in_=groups[b][:, lo * 1024 : hi * 1024],
            )

        def store(s, j0, j1):
            nc.sync.dma_start(out=ov[s][:, j0 * D_OUT : j1 * D_OUT], in_=o_tiles[s][:, j0 * D_OUT : j1 * D_OUT])

        def passes(b, i):
            rt = bunches[b][i]
            s, j = divmod(rt, J)
            if j == 0:
                o_slab = slabs.tile([P, J * D_OUT], F32, name="o_slab", tag="slab%d" % s)
                o_tiles[s] = o_slab
            xc, xs = codes[b]
            ob = bank([P, D_OUT], F32)
            for g in range(2):
                m_cols = slice((2 * i + g) * P, (2 * i + g + 1) * P)
                n_cols = slice(g * D_OUT, (g + 1) * D_OUT)
                nc.tensor.matmul_mx(
                    out=ob[:],
                    lhsT=xc[:, m_cols].bitcast(FP8X4),
                    lhsT_scale=xs[:, m_cols],
                    rhs=wc[:, n_cols].bitcast(FP8X4),
                    rhs_scale=ws[:, n_cols],
                    start=(g == 0),
                    stop=(g == 1),
                )
            o_cols = o_tiles[s][:, j * D_OUT : (j + 1) * D_OUT]
            nc.vector.tensor_tensor(out=o_cols, in0=ob[:], in1=bias_sb[:], op=ADD)
            step = STORE_STEPS[s]
            if (j + 1) % step == 0:
                store(s, j + 1 - step, j + 1)

        for t in range(4):
            weight_transposes(t)
        sort_words(0)
        transposes(0)
        weight_quantise(0)
        weight_quantise(1)
        sort_words(1)
        for piece in pieces(0):
            quantise(0, piece)
        pb = bank([P, D_OUT], F32)
        nc.tensor.matmul(pb[:], lhsT=ones[:], rhs=bias_row[:], start=True, stop=True)
        nc.scalar.copy(out=bias_sb[:], in_=pb[:])
        transposes(1)
        sort_words(2)

        for b in range(len(bunches)):
            todo = pieces(b + 1) if b + 1 < len(bunches) else []
            if b + 2 < len(bunches):
                for i in range(len(bunches[b])):
                    passes(b, i)
                for piece in todo:
                    quantise(b + 1, piece)
                transposes(b + 2)
                sort_words(b + 3)
            else:
                for i in range(len(bunches[b])):
                    if i < len(todo):
                        quantise(b + 1, todo[i])
                    passes(b, i)
